import numpy as np
import ml_dtypes


def mxq(x, axis, fmt="e4m3"):
    dtype, down = {"e4m3": (ml_dtypes.float8_e4m3fn, 7), "e5m2": (ml_dtypes.float8_e5m2, 14)}[fmt]
    v = np.moveaxis(np.asarray(x, np.float32).astype(ml_dtypes.bfloat16).astype(np.float64), axis, -1)
    blocks = v.reshape(v.shape[:-1] + (-1, 32))
    amax = np.abs(blocks).max(-1, keepdims=True)
    byte = np.maximum(np.where(amax > 0, np.frexp(amax)[1] - 1 + 127, 0) - down, 1)
    scale = np.exp2(byte - 127.0)
    codes = (blocks / scale).astype(np.float32).astype(dtype).astype(np.float64)
    return np.moveaxis((codes * scale).reshape(v.shape), -1, axis)


WIDE = False


def mx_kscale(k):
    if not WIDE:
        return np.ones(k)
    levels = np.array([10, -10, 5, -5, 0])
    a = np.random.permutation(np.resize(levels, k // 512 * 4)).reshape(k // 512, 4)
    idx = np.arange(k)
    return np.exp2(a[idx // 512, idx % 128 // 32])


BF16 = ml_dtypes.bfloat16


def bf(x):
    return np.asarray(x, np.float32).astype(BF16)


def f64(x):
    return np.asarray(x).astype(np.float64)


B, Q, P, H1, H2, C, GN, KO = 4096, 7, 4, 512, 256, 256, 5, 3
NB = GN + KO
LO, HI = -2.0, 2.0


def mish(v):
    return v * np.tanh(np.logaddexp(0.0, v))


def bspline_basis(v):
    step = (HI - LO) / GN
    knots = LO + step * np.arange(-KO, GN + KO + 1)
    vv = v[..., None]
    bas = np.where((vv >= knots[:-1]) & (vv < knots[1:]), 1.0, 0.0)
    for d in range(1, KO + 1):
        left = (vv - knots[: -(d + 1)]) / (knots[d:-1] - knots[: -(d + 1)]) * bas[..., :-1]
        right = (knots[d + 1:] - vv) / (knots[d + 1:] - knots[1:-d]) * bas[..., 1:]
        bas = left + right
    return bas


def setup_inputs():
    t = np.minimum(mx_kscale(H1), 1.0) ** 2
    return {'h1': bf(np.random.standard_normal((B, H1)) * t),
            'coef2': bf(np.random.standard_normal((H1, H2, NB)) / np.sqrt(H1)),
            'sb2': bf(np.random.standard_normal((H1, H2)) / np.sqrt(H1) / t[:, None]),
            'sp2': bf(1.0 + 0.3 * np.random.standard_normal((H1, H2))),
            'b2': bf(0.2 * np.random.standard_normal(H2))}


def reference(h1, coef2, sb2, sp2, b2):
    x = f64(h1)
    phi = bspline_basis(x).transpose(2, 0, 1)
    w = (f64(coef2) * f64(sp2)[..., None]).transpose(2, 0, 1)
    spline = (mxq(phi, 2, 'e4m3') @ mxq(w, 1, 'e4m3')).sum(0)
    base = mxq(mish(x), 1, 'e4m3') @ mxq(f64(sb2), 0, 'e4m3')
    return base + spline + f64(b2)

@@ -1,0 +1,153 @@
+import math
+from contextlib import ExitStack
+
+import concourse.mybir as mybir
+from concourse.masks import make_identity
+
+BF16 = mybir.dt.bfloat16
+F32 = mybir.dt.float32
+U32 = mybir.dt.uint32
+U8 = mybir.dt.uint8
+FP8X4 = mybir.dt.float8_e4m3fn_x4
+ACT = mybir.ActivationFunctionType
+ALU = mybir.AluOpType
+
+P = 128
+PACK = 4
+BATCH, FEATURES, OUTPUTS, BASIS = 4096, 512, 256, 8
+PLANES = BASIS + 1
+MISH = BASIS
+PAIRS = BASIS // 2
+TILES = 4
+CHUNK_ROWS = TILES * P
+CHUNKS = BATCH // CHUNK_ROWS
+COLS = TILES * FEATURES
+WORDS = COLS // PACK
+
+FLOPS = 2 * BATCH * OUTPUTS * PLANES * FEATURES
+
+
+def tile_net_pa_t_kernel(tc, h1, coef2, sb2, sp2, b2, out):
+    nc = tc.nc
+    with ExitStack() as stack:
+        keep = stack.enter_context(tc.tile_pool(name="keep", bufs=1))
+        io = stack.enter_context(tc.tile_pool(name="io", bufs=2))
+        work = stack.enter_context(tc.tile_pool(name="work", bufs=2))
+        turn_banks = stack.enter_context(tc.psum_pool(name="turn_banks", bufs=2))
+        sum_banks = stack.enter_context(tc.psum_pool(name="sum_banks", bufs=4))
+
+        identity = keep.tile([P, P], F32)
+        make_identity(nc, identity[:])
+
+        shifts = keep.tile([P, PAIRS + 2], F32)
+        for r in range(PAIRS):
+            nc.vector.memset(shifts[:, r : r + 1], 1.5 - r)
+        nc.vector.memset(shifts[:, PAIRS : PAIRS + 1], -2.0)
+        nc.vector.memset(shifts[:, PAIRS + 1 : PAIRS + 2], 1.0)
+        minus_two = shifts[:, PAIRS : PAIRS + 1]
+        plus_one = shifts[:, PAIRS + 1 : PAIRS + 2]
+
+        bias = keep.tile([P, OUTPUTS], BF16)
+        nc.sync.dma_start(out=bias[:], in_=b2.partition_broadcast(P))
+
+        w_codes = keep.tile([P, PLANES, OUTPUTS], U32, align_bytes=64)
+        w_scales = keep.tile([P, PLANES, OUTPUTS], U8, align_bytes=64)
+        with tc.tile_pool(name="wprep", bufs=1) as wprep:
+            coef_rows = wprep.tile([P, PACK, OUTPUTS * BASIS], BF16)
+            nc.sync.dma_start(out=coef_rows[:], in_=coef2.rearrange("(p j) o g -> p j (o g)", j=PACK))
+            gain_rows = wprep.tile([P, PACK, OUTPUTS], BF16)
+            nc.sync.dma_start(out=gain_rows[:], in_=sp2.rearrange("(p j) o -> p j o", j=PACK))
+            base_rows = wprep.tile([P, PACK, OUTPUTS], BF16)
+            nc.sync.dma_start(out=base_rows[:], in_=sb2.rearrange("(p j) o -> p j o", j=PACK))
+            w_grouped = wprep.tile([P, PLANES, OUTPUTS, PACK], BF16, align_bytes=64)
+            coef_by_plane = coef_rows[:].rearrange("p j (o g) -> p g o j", g=BASIS)
+            for g in range(BASIS):
+                nc.vector.tensor_tensor(
+                    out=w_grouped[:, g],
+                    in0=coef_by_plane[:, g],
+                    in1=gain_rows[:].rearrange("p j o -> p o j"),
+                    op=ALU.mult,
+                )
+            nc.vector.tensor_copy(out=w_grouped[:, MISH], in_=base_rows[:].rearrange("p j o -> p o j"))
+            for plane in range(PLANES):
+                nc.vector.quantize_mx(
+                    out=w_codes[:, plane, :].bitcast(FP8X4),
+                    scales=w_scales[:, plane, :],
+                    in_=w_grouped[:, plane].rearrange("p o j -> p (o j)"),
+                )
+
+        halves = stack.enter_context(tc.tile_pool(name="halves", bufs=2))
+        quant = stack.enter_context(tc.tile_pool(name="quant", bufs=2))
+        results = stack.enter_context(tc.tile_pool(name="results", bufs=2))
+
+        for c in range(CHUNKS):
+            rows = slice(c * CHUNK_ROWS, (c + 1) * CHUNK_ROWS)
+
+            raw = io.tile([P, COLS], BF16)
+            nc.sync.dma_start(out=raw[:], in_=h1[rows, :].rearrange("(p t) i -> p (t i)", t=TILES))
+            raw_words = raw[:].bitcast(F32).rearrange("p (t w u) -> p t u w", t=TILES, u=2)
+            x = io.tile([P, COLS], BF16, align_bytes=64)
+            x_words = x[:].bitcast(F32).rearrange("p (h t b u) -> p h t b u", h=2, t=2, u=2)
+            for h in range(2):
+                turned = turn_banks.tile([P, 2, 2, P], F32)
+                for t in range(2):
+                    for u in range(2):
+                        nc.tensor.transpose(turned[:, t, u, :], raw_words[:, 2 * h + t, u, :], identity[:])
+                nc.scalar.copy(out=x_words[:, h], in_=turned[:].rearrange("p t u b -> p t b u"))
+
+            codes = quant.tile([P, PLANES, WORDS], U32, align_bytes=64)
+            scales = quant.tile([P, PLANES, WORDS], U8, align_bytes=64)
+
+            for r in range(PAIRS):
+                dist = work.tile([P, COLS], F32)
+                nc.scalar.activation(out=dist[:], in_=x[:], func=ACT.Abs, scale=1.25, bias=shifts[:, r : r + 1])
+                nc.scalar.activation(out=dist[:], in_=dist[:], func=ACT.Abs, bias=minus_two)
+                wide = work.tile([P, COLS], F32)
+                nc.vector.tensor_scalar(out=wide[:], in0=dist[:], scalar1=2.0, scalar2=-2.0, op0=ALU.min, op1=ALU.add)
+                narrow = work.tile([P, COLS], F32)
+                nc.vector.tensor_scalar(out=narrow[:], in0=dist[:], scalar1=1.0, scalar2=-1.0, op0=ALU.min, op1=ALU.add)
+                wide_sq = work.tile([P, COLS], F32)
+                nc.scalar.activation(out=wide_sq[:], in_=wide[:], func=ACT.Square, scale=math.sqrt(1.0 / 6.0))
+                narrow_sq = work.tile([P, COLS], F32)
+                nc.scalar.activation(out=narrow_sq[:], in_=narrow[:], func=ACT.Square, scale=math.sqrt(2.0 / 3.0))
+                nc.vector.tensor_tensor(out=wide_sq[:], in0=wide_sq[:], in1=wide[:], op=ALU.mult)
+                nc.vector.tensor_tensor(out=narrow_sq[:], in0=narrow_sq[:], in1=narrow[:], op=ALU.mult)
+                both = halves.tile([P, COLS], BF16)
+                nc.vector.tensor_tensor(out=both[:], in0=narrow_sq[:], in1=wide_sq[:], op=ALU.subtract)
+                below = halves.tile([P, COLS], BF16)
+                nc.vector.tensor_single_scalar(out=below[:], in_=x[:], scalar=0.8 * r - 1.2, op=ALU.is_lt)
+                low = halves.tile([P, COLS], BF16, align_bytes=64)
+                nc.vector.tensor_tensor(out=low[:], in0=both[:], in1=below[:], op=ALU.mult)
+                high = halves.tile([P, COLS], BF16, align_bytes=64)
+                nc.vector.tensor_tensor(out=high[:], in0=both[:], in1=low[:], op=ALU.subtract)
+                nc.vector.quantize_mx(out=codes[:, r, :].bitcast(FP8X4), scales=scales[:, r, :], in_=low[:])
+                nc.vector.quantize_mx(
+                    out=codes[:, r + PAIRS, :].bitcast(FP8X4), scales=scales[:, r + PAIRS, :], in_=high[:]
+                )
+
+            capped = halves.tile([P, COLS], BF16)
+            nc.vector.tensor_scalar_min(out=capped[:], in0=x[:], scalar1=20.0)
+            soft = work.tile([P, COLS], F32)
+            nc.scalar.activation(out=soft[:], in_=capped[:], func=ACT.Exp)
+            nc.scalar.activation(out=soft[:], in_=soft[:], func=ACT.Ln, bias=plus_one)
+            nc.scalar.activation(out=soft[:], in_=soft[:], func=ACT.Tanh)
+            mish = halves.tile([P, COLS], BF16, align_bytes=64)
+            nc.vector.tensor_tensor(out=mish[:], in0=x[:], in1=soft[:], op=ALU.mult)
+            nc.vector.quantize_mx(out=codes[:, MISH, :].bitcast(FP8X4), scales=scales[:, MISH, :], in_=mish[:])
+
+            result = results.tile([P, TILES, OUTPUTS], F32)
+            for t in range(TILES):
+                cols = slice(t * P, (t + 1) * P)
+                acc = sum_banks.tile([P, OUTPUTS], F32)
+                for plane in range(PLANES):
+                    nc.tensor.matmul_mx(
+                        out=acc[:],
+                        lhsT=codes[:, plane, cols].bitcast(FP8X4),
+                        lhsT_scale=scales[:, plane, cols],
+                        rhs=w_codes[:, plane, :].bitcast(FP8X4),
+                        rhs_scale=w_scales[:, plane, :],
+                        start=(plane == 0),
+                        stop=(plane == PLANES - 1),
+                    )
+                nc.vector.tensor_tensor(out=result[:, t, :], in0=acc[:], in1=bias[:], op=ALU.add)
+            nc.sync.dma_start(out=out[rows, :].rearrange("(p t) o -> p t o", t=TILES), in_=result[:])

@@ -1,4 +1,3 @@
-import math
 from contextlib import ExitStack
 
 import concourse.mybir as mybir
@@ -103,17 +102,22 @@ def tile_net_pa_t_kernel(tc, h1, coef2, sb2, sp2, b2, out):
                 nc.scalar.activation(out=dist[:], in_=x[:], func=ACT.Abs, scale=1.25, bias=shifts[:, r : r + 1])
                 nc.scalar.activation(out=dist[:], in_=dist[:], func=ACT.Abs, bias=minus_two)
                 wide = work.tile([P, COLS], F32)
-                nc.vector.tensor_scalar(out=wide[:], in0=dist[:], scalar1=2.0, scalar2=-2.0, op0=ALU.min, op1=ALU.add)
+                nc.scalar.activation(out=wide[:], in_=dist[:], func=ACT.Square, bias=minus_two)
                 narrow = work.tile([P, COLS], F32)
-                nc.vector.tensor_scalar(out=narrow[:], in0=dist[:], scalar1=1.0, scalar2=-1.0, op0=ALU.min, op1=ALU.add)
-                wide_sq = work.tile([P, COLS], F32)
-                nc.scalar.activation(out=wide_sq[:], in_=wide[:], func=ACT.Square, scale=math.sqrt(1.0 / 6.0))
-                narrow_sq = work.tile([P, COLS], F32)
-                nc.scalar.activation(out=narrow_sq[:], in_=narrow[:], func=ACT.Square, scale=math.sqrt(2.0 / 3.0))
-                nc.vector.tensor_tensor(out=wide_sq[:], in0=wide_sq[:], in1=wide[:], op=ALU.mult)
-                nc.vector.tensor_tensor(out=narrow_sq[:], in0=narrow_sq[:], in1=narrow[:], op=ALU.mult)
+                nc.scalar.activation(out=narrow[:], in_=dist[:], func=ACT.Square, scale=2.0, bias=minus_two)
+                nc.vector.scalar_tensor_tensor(
+                    out=wide[:], in0=dist[:], scalar=-2.0, in1=wide[:], op0=ALU.add, op1=ALU.mult
+                )
+                nc.vector.scalar_tensor_tensor(
+                    out=narrow[:], in0=dist[:], scalar=-1.0, in1=narrow[:], op0=ALU.add, op1=ALU.mult
+                )
+                nc.vector.scalar_tensor_tensor(
+                    out=wide[:], in0=narrow[:], scalar=0.0, in1=wide[:], op0=ALU.min, op1=ALU.subtract
+                )
                 both = halves.tile([P, COLS], BF16)
-                nc.vector.tensor_tensor(out=both[:], in0=narrow_sq[:], in1=wide_sq[:], op=ALU.subtract)
+                nc.vector.tensor_scalar(
+                    out=both[:], in0=wide[:], scalar1=0.0, scalar2=1.0 / 6.0, op0=ALU.max, op1=ALU.mult
+                )
                 below = halves.tile([P, COLS], BF16)
                 nc.vector.tensor_single_scalar(out=below[:], in_=x[:], scalar=0.8 * r - 1.2, op=ALU.is_lt)
                 low = halves.tile([P, COLS], BF16, align_bytes=64)

@@ -1,3 +1,4 @@
+import math
 from contextlib import ExitStack
 
 import concourse.mybir as mybir
@@ -16,12 +17,16 @@ PACK = 4
 BATCH, FEATURES, OUTPUTS, BASIS = 4096, 512, 256, 8
 PLANES = BASIS + 1
 MISH = BASIS
+FIRST_PLANE, LAST_PLANE = MISH, BASIS - 1
 PAIRS = BASIS // 2
 TILES = 4
 CHUNK_ROWS = TILES * P
 CHUNKS = BATCH // CHUNK_ROWS
 COLS = TILES * FEATURES
 WORDS = COLS // PACK
+
+ROOT = round(math.sqrt(1.0 / 6.0) * 2**25) / 2**25
+MAKE_UP = 1.0 / (6.0 * ROOT * ROOT)
 
 FLOPS = 2 * BATCH * OUTPUTS * PLANES * FEATURES
 
@@ -33,18 +38,20 @@ def tile_net_pa_t_kernel(tc, h1, coef2, sb2, sp2, b2, out):
         io = stack.enter_context(tc.tile_pool(name="io", bufs=2))
         work = stack.enter_context(tc.tile_pool(name="work", bufs=2))
         turn_banks = stack.enter_context(tc.psum_pool(name="turn_banks", bufs=2))
-        sum_banks = stack.enter_context(tc.psum_pool(name="sum_banks", bufs=4))
+        sum_banks = stack.enter_context(tc.psum_pool(name="sum_banks", bufs=1))
 
         identity = keep.tile([P, P], F32)
         make_identity(nc, identity[:])
 
-        shifts = keep.tile([P, PAIRS + 2], F32)
+        shifts = keep.tile([P, PAIRS + 3], F32)
         for r in range(PAIRS):
             nc.vector.memset(shifts[:, r : r + 1], 1.5 - r)
         nc.vector.memset(shifts[:, PAIRS : PAIRS + 1], -2.0)
         nc.vector.memset(shifts[:, PAIRS + 1 : PAIRS + 2], 1.0)
         minus_two = shifts[:, PAIRS : PAIRS + 1]
         plus_one = shifts[:, PAIRS + 1 : PAIRS + 2]
+        nc.vector.memset(shifts[:, PAIRS + 2 : PAIRS + 3], -2.0 * ROOT)
+        minus_two_roots = shifts[:, PAIRS + 2 : PAIRS + 3]
 
         bias = keep.tile([P, OUTPUTS], BF16)
         nc.sync.dma_start(out=bias[:], in_=b2.partition_broadcast(P))
@@ -96,38 +103,23 @@ def tile_net_pa_t_kernel(tc, h1, coef2, sb2, sp2, b2, out):
 
             codes = quant.tile([P, PLANES, WORDS], U32, align_bytes=64)
             scales = quant.tile([P, PLANES, WORDS], U8, align_bytes=64)
+            sums = [sum_banks.tile([P, OUTPUTS], F32, name="sum%d" % t) for t in range(TILES)]
 
-            for r in range(PAIRS):
-                dist = work.tile([P, COLS], F32)
-                nc.scalar.activation(out=dist[:], in_=x[:], func=ACT.Abs, scale=1.25, bias=shifts[:, r : r + 1])
-                nc.scalar.activation(out=dist[:], in_=dist[:], func=ACT.Abs, bias=minus_two)
-                wide = work.tile([P, COLS], F32)
-                nc.scalar.activation(out=wide[:], in_=dist[:], func=ACT.Square, bias=minus_two)
-                narrow = work.tile([P, COLS], F32)
-                nc.scalar.activation(out=narrow[:], in_=dist[:], func=ACT.Square, scale=2.0, bias=minus_two)
-                nc.vector.scalar_tensor_tensor(
-                    out=wide[:], in0=dist[:], scalar=-2.0, in1=wide[:], op0=ALU.add, op1=ALU.mult
-                )
-                nc.vector.scalar_tensor_tensor(
-                    out=narrow[:], in0=dist[:], scalar=-1.0, in1=narrow[:], op0=ALU.add, op1=ALU.mult
-                )
-                nc.vector.scalar_tensor_tensor(
-                    out=wide[:], in0=narrow[:], scalar=0.0, in1=wide[:], op0=ALU.min, op1=ALU.subtract
-                )
-                both = halves.tile([P, COLS], BF16)
-                nc.vector.tensor_scalar(
-                    out=both[:], in0=wide[:], scalar1=0.0, scalar2=1.0 / 6.0, op0=ALU.max, op1=ALU.mult
-                )
-                below = halves.tile([P, COLS], BF16)
-                nc.vector.tensor_single_scalar(out=below[:], in_=x[:], scalar=0.8 * r - 1.2, op=ALU.is_lt)
-                low = halves.tile([P, COLS], BF16, align_bytes=64)
-                nc.vector.tensor_tensor(out=low[:], in0=both[:], in1=below[:], op=ALU.mult)
-                high = halves.tile([P, COLS], BF16, align_bytes=64)
-                nc.vector.tensor_tensor(out=high[:], in0=both[:], in1=low[:], op=ALU.subtract)
-                nc.vector.quantize_mx(out=codes[:, r, :].bitcast(FP8X4), scales=scales[:, r, :], in_=low[:])
+            def quantise_and_multiply(plane, values):
                 nc.vector.quantize_mx(
-                    out=codes[:, r + PAIRS, :].bitcast(FP8X4), scales=scales[:, r + PAIRS, :], in_=high[:]
+                    out=codes[:, plane, :].bitcast(FP8X4), scales=scales[:, plane, :], in_=values
                 )
+                for t in range(TILES):
+                    cols = slice(t * P, (t + 1) * P)
+                    nc.tensor.matmul_mx(
+                        out=sums[t][:],
+                        lhsT=codes[:, plane, cols].bitcast(FP8X4),
+                        lhsT_scale=scales[:, plane, cols],
+                        rhs=w_codes[:, plane, :].bitcast(FP8X4),
+                        rhs_scale=w_scales[:, plane, :],
+                        start=(plane == FIRST_PLANE),
+                        stop=(plane == LAST_PLANE),
+                    )
 
             capped = halves.tile([P, COLS], BF16)
             nc.vector.tensor_scalar_min(out=capped[:], in0=x[:], scalar1=20.0)
@@ -137,21 +129,41 @@ def tile_net_pa_t_kernel(tc, h1, coef2, sb2, sp2, b2, out):
             nc.scalar.activation(out=soft[:], in_=soft[:], func=ACT.Tanh)
             mish = halves.tile([P, COLS], BF16, align_bytes=64)
             nc.vector.tensor_tensor(out=mish[:], in0=x[:], in1=soft[:], op=ALU.mult)
-            nc.vector.quantize_mx(out=codes[:, MISH, :].bitcast(FP8X4), scales=scales[:, MISH, :], in_=mish[:])
+            quantise_and_multiply(MISH, mish[:])
+
+            for r in range(PAIRS):
+                dist = work.tile([P, COLS], F32)
+                nc.scalar.activation(out=dist[:], in_=x[:], func=ACT.Abs, scale=1.25, bias=shifts[:, r : r + 1])
+                nc.scalar.activation(out=dist[:], in_=dist[:], func=ACT.Abs, bias=minus_two)
+                wide = work.tile([P, COLS], F32)
+                nc.scalar.activation(out=wide[:], in_=dist[:], func=ACT.Square, scale=ROOT, bias=minus_two_roots)
+                narrow = work.tile([P, COLS], F32)
+                nc.scalar.activation(
+                    out=narrow[:], in_=dist[:], func=ACT.Square, scale=2.0 * ROOT, bias=minus_two_roots
+                )
+                nc.vector.scalar_tensor_tensor(
+                    out=wide[:], in0=dist[:], scalar=-2.0, in1=wide[:], op0=ALU.add, op1=ALU.mult
+                )
+                nc.vector.scalar_tensor_tensor(
+                    out=narrow[:], in0=dist[:], scalar=-1.0, in1=narrow[:], op0=ALU.add, op1=ALU.mult
+                )
+                both = halves.tile([P, COLS], BF16)
+                nc.vector.scalar_tensor_tensor(
+                    out=both[:], in0=narrow[:], scalar=0.0, in1=wide[:], op0=ALU.min, op1=ALU.subtract
+                )
+                nc.vector.tensor_scalar(
+                    out=both[:], in0=both[:], scalar1=0.0, scalar2=MAKE_UP, op0=ALU.max, op1=ALU.mult
+                )
+                below = halves.tile([P, COLS], BF16)
+                nc.vector.tensor_single_scalar(out=below[:], in_=x[:], scalar=0.8 * r - 1.2, op=ALU.is_lt)
+                low = halves.tile([P, COLS], BF16, align_bytes=64)
+                nc.vector.tensor_tensor(out=low[:], in0=both[:], in1=below[:], op=ALU.mult)
+                high = halves.tile([P, COLS], BF16, align_bytes=64)
+                nc.vector.tensor_tensor(out=high[:], in0=both[:], in1=low[:], op=ALU.subtract)
+                quantise_and_multiply(r, low[:])
+                quantise_and_multiply(r + PAIRS, high[:])
 
             result = results.tile([P, TILES, OUTPUTS], F32)
             for t in range(TILES):
-                cols = slice(t * P, (t + 1) * P)
-                acc = sum_banks.tile([P, OUTPUTS], F32)
-                for plane in range(PLANES):
-                    nc.tensor.matmul_mx(
-                        out=acc[:],
-                        lhsT=codes[:, plane, cols].bitcast(FP8X4),
-                        lhsT_scale=scales[:, plane, cols],
-                        rhs=w_codes[:, plane, :].bitcast(FP8X4),
-                        rhs_scale=w_scales[:, plane, :],
-                        start=(plane == 0),
-                        stop=(plane == PLANES - 1),
-                    )
-                nc.vector.tensor_tensor(out=result[:, t, :], in0=acc[:], in1=bias[:], op=ALU.add)
+                nc.vector.tensor_tensor(out=result[:, t, :], in0=sums[t][:], in1=bias[:], op=ALU.add)
             nc.sync.dma_start(out=out[rows, :].rearrange("(p t) o -> p t o", t=TILES), in_=result[:])

@@ -54,17 +54,17 @@ def tile_net_pa_t_kernel(tc, h1, coef2, sb2, sp2, b2, out):
         minus_two_roots = shifts[:, PAIRS + 2 : PAIRS + 3]
 
         bias = keep.tile([P, OUTPUTS], BF16)
-        nc.sync.dma_start(out=bias[:], in_=b2.partition_broadcast(P))
+        nc.scalar.dma_start(out=bias[:], in_=b2.partition_broadcast(P))
 
         w_codes = keep.tile([P, PLANES, OUTPUTS], U32, align_bytes=64)
         w_scales = keep.tile([P, PLANES, OUTPUTS], U8, align_bytes=64)
         with tc.tile_pool(name="wprep", bufs=1) as wprep:
             coef_rows = wprep.tile([P, PACK, OUTPUTS * BASIS], BF16)
-            nc.sync.dma_start(out=coef_rows[:], in_=coef2.rearrange("(p j) o g -> p j (o g)", j=PACK))
+            nc.scalar.dma_start(out=coef_rows[:], in_=coef2.rearrange("(p j) o g -> p j (o g)", j=PACK))
             gain_rows = wprep.tile([P, PACK, OUTPUTS], BF16)
-            nc.sync.dma_start(out=gain_rows[:], in_=sp2.rearrange("(p j) o -> p j o", j=PACK))
+            nc.scalar.dma_start(out=gain_rows[:], in_=sp2.rearrange("(p j) o -> p j o", j=PACK))
             base_rows = wprep.tile([P, PACK, OUTPUTS], BF16)
-            nc.sync.dma_start(out=base_rows[:], in_=sb2.rearrange("(p j) o -> p j o", j=PACK))
+            nc.scalar.dma_start(out=base_rows[:], in_=sb2.rearrange("(p j) o -> p j o", j=PACK))
             w_grouped = wprep.tile([P, PLANES, OUTPUTS, PACK], BF16, align_bytes=64)
             coef_by_plane = coef_rows[:].rearrange("p j (o g) -> p g o j", g=BASIS)
             for g in range(BASIS):
@@ -86,6 +86,43 @@ def tile_net_pa_t_kernel(tc, h1, coef2, sb2, sp2, b2, out):
         quant = stack.enter_context(tc.tile_pool(name="quant", bufs=2))
         results = stack.enter_context(tc.tile_pool(name="results", bufs=2))
 
+        def quantise_and_multiply(chunk, plane, values):
+            codes, scales, sums = chunk["codes"], chunk["scales"], chunk["sums"]
+            nc.vector.quantize_mx(out=codes[:, plane, :].bitcast(FP8X4), scales=scales[:, plane, :], in_=values)
+            for t in range(TILES):
+                cols = slice(t * P, (t + 1) * P)
+                nc.tensor.matmul_mx(
+                    out=sums[t][:],
+                    lhsT=codes[:, plane, cols].bitcast(FP8X4),
+                    lhsT_scale=scales[:, plane, cols],
+                    rhs=w_codes[:, plane, :].bitcast(FP8X4),
+                    rhs_scale=w_scales[:, plane, :],
+                    start=(plane == FIRST_PLANE),
+                    stop=(plane == LAST_PLANE),
+                )
+
+        def end_at_zero(pair):
+            nc.vector.tensor_scalar(
+                out=pair["both"][:], in0=pair["both"][:], scalar1=0.0, scalar2=MAKE_UP, op0=ALU.max, op1=ALU.mult
+            )
+
+        def take_low(pair):
+            nc.vector.tensor_tensor(out=pair["low"][:], in0=pair["both"][:], in1=pair["below"][:], op=ALU.mult)
+
+        def take_high(pair):
+            nc.vector.tensor_tensor(out=pair["high"][:], in0=pair["both"][:], in1=pair["low"][:], op=ALU.subtract)
+
+        def finish(pair):
+            chunk, r = pair["chunk"], pair["r"]
+            quantise_and_multiply(chunk, r, pair["low"][:])
+            quantise_and_multiply(chunk, r + PAIRS, pair["high"][:])
+            if r == PAIRS - 1:
+                result = results.tile([P, TILES, OUTPUTS], F32)
+                for t in range(TILES):
+                    nc.vector.tensor_tensor(out=result[:, t, :], in0=chunk["sums"][t][:], in1=bias[:], op=ALU.add)
+                nc.sync.dma_start(out=out[chunk["rows"], :].rearrange("(p t) o -> p t o", t=TILES), in_=result[:])
+
+        earlier = None
         for c in range(CHUNKS):
             rows = slice(c * CHUNK_ROWS, (c + 1) * CHUNK_ROWS)
 
@@ -101,25 +138,12 @@ def tile_net_pa_t_kernel(tc, h1, coef2, sb2, sp2, b2, out):
                         nc.tensor.transpose(turned[:, t, u, :], raw_words[:, 2 * h + t, u, :], identity[:])
                 nc.scalar.copy(out=x_words[:, h], in_=turned[:].rearrange("p t u b -> p t b u"))
 
-            codes = quant.tile([P, PLANES, WORDS], U32, align_bytes=64)
-            scales = quant.tile([P, PLANES, WORDS], U8, align_bytes=64)
-            sums = [sum_banks.tile([P, OUTPUTS], F32, name="sum%d" % t) for t in range(TILES)]
-
-            def quantise_and_multiply(plane, values):
-                nc.vector.quantize_mx(
-                    out=codes[:, plane, :].bitcast(FP8X4), scales=scales[:, plane, :], in_=values
-                )
-                for t in range(TILES):
-                    cols = slice(t * P, (t + 1) * P)
-                    nc.tensor.matmul_mx(
-                        out=sums[t][:],
-                        lhsT=codes[:, plane, cols].bitcast(FP8X4),
-                        lhsT_scale=scales[:, plane, cols],
-                        rhs=w_codes[:, plane, :].bitcast(FP8X4),
-                        rhs_scale=w_scales[:, plane, :],
-                        start=(plane == FIRST_PLANE),
-                        stop=(plane == LAST_PLANE),
-                    )
+            chunk = {
+                "rows": rows,
+                "codes": quant.tile([P, PLANES, WORDS], U32, align_bytes=64, name="codes"),
+                "scales": quant.tile([P, PLANES, WORDS], U8, align_bytes=64, name="scales"),
+                "sums": [sum_banks.tile([P, OUTPUTS], F32, name="sum%d" % t) for t in range(TILES)],
+            }
 
             capped = halves.tile([P, COLS], BF16)
             nc.vector.tensor_scalar_min(out=capped[:], in0=x[:], scalar1=20.0)
@@ -128,8 +152,6 @@ def tile_net_pa_t_kernel(tc, h1, coef2, sb2, sp2, b2, out):
             nc.scalar.activation(out=soft[:], in_=soft[:], func=ACT.Ln, bias=plus_one)
             nc.scalar.activation(out=soft[:], in_=soft[:], func=ACT.Tanh)
             mish = halves.tile([P, COLS], BF16, align_bytes=64)
-            nc.vector.tensor_tensor(out=mish[:], in0=x[:], in1=soft[:], op=ALU.mult)
-            quantise_and_multiply(MISH, mish[:])
 
             for r in range(PAIRS):
                 dist = work.tile([P, COLS], F32)
@@ -141,29 +163,39 @@ def tile_net_pa_t_kernel(tc, h1, coef2, sb2, sp2, b2, out):
                 nc.scalar.activation(
                     out=narrow[:], in_=dist[:], func=ACT.Square, scale=2.0 * ROOT, bias=minus_two_roots
                 )
+                pair = {
+                    "chunk": chunk,
+                    "r": r,
+                    "both": halves.tile([P, COLS], BF16, name="both"),
+                    "below": halves.tile([P, COLS], BF16, name="below"),
+                    "low": halves.tile([P, COLS], BF16, align_bytes=64, name="low"),
+                    "high": halves.tile([P, COLS], BF16, align_bytes=64, name="high"),
+                }
                 nc.vector.scalar_tensor_tensor(
                     out=wide[:], in0=dist[:], scalar=-2.0, in1=wide[:], op0=ALU.add, op1=ALU.mult
                 )
+                if earlier is not None:
+                    end_at_zero(earlier)
                 nc.vector.scalar_tensor_tensor(
                     out=narrow[:], in0=dist[:], scalar=-1.0, in1=narrow[:], op0=ALU.add, op1=ALU.mult
                 )
-                both = halves.tile([P, COLS], BF16)
+                if earlier is not None:
+                    take_low(earlier)
+                nc.vector.tensor_single_scalar(out=pair["below"][:], in_=x[:], scalar=0.8 * r - 1.2, op=ALU.is_lt)
+                if earlier is not None:
+                    take_high(earlier)
                 nc.vector.scalar_tensor_tensor(
-                    out=both[:], in0=narrow[:], scalar=0.0, in1=wide[:], op0=ALU.min, op1=ALU.subtract
+                    out=pair["both"][:], in0=narrow[:], scalar=0.0, in1=wide[:], op0=ALU.min, op1=ALU.subtract
                 )
-                nc.vector.tensor_scalar(
-                    out=both[:], in0=both[:], scalar1=0.0, scalar2=MAKE_UP, op0=ALU.max, op1=ALU.mult
-                )
-                below = halves.tile([P, COLS], BF16)
-                nc.vector.tensor_single_scalar(out=below[:], in_=x[:], scalar=0.8 * r - 1.2, op=ALU.is_lt)
-                low = halves.tile([P, COLS], BF16, align_bytes=64)
-                nc.vector.tensor_tensor(out=low[:], in0=both[:], in1=below[:], op=ALU.mult)
-                high = halves.tile([P, COLS], BF16, align_bytes=64)
-                nc.vector.tensor_tensor(out=high[:], in0=both[:], in1=low[:], op=ALU.subtract)
-                quantise_and_multiply(r, low[:])
-                quantise_and_multiply(r + PAIRS, high[:])
+                if r == 0:
+                    nc.vector.tensor_tensor(out=mish[:], in0=x[:], in1=soft[:], op=ALU.mult)
+                if earlier is not None:
+                    finish(earlier)
+                if r == 0:
+                    quantise_and_multiply(chunk, MISH, mish[:])
+                earlier = pair
 
-            result = results.tile([P, TILES, OUTPUTS], F32)
-            for t in range(TILES):
-                nc.vector.tensor_tensor(out=result[:, t, :], in0=sums[t][:], in1=bias[:], op=ALU.add)
-            nc.sync.dma_start(out=out[rows, :].rearrange("(p t) o -> p t o", t=TILES), in_=result[:])
+        end_at_zero(earlier)
+        take_low(earlier)
+        take_high(earlier)
+        finish(earlier)

import math
from contextlib import ExitStack

import concourse.mybir as mybir
from concourse.masks import make_identity

BF16 = mybir.dt.bfloat16
F32 = mybir.dt.float32
U32 = mybir.dt.uint32
U8 = mybir.dt.uint8
FP8X4 = mybir.dt.float8_e4m3fn_x4
ACT = mybir.ActivationFunctionType
ALU = mybir.AluOpType

P = 128
PACK = 4
BATCH, FEATURES, OUTPUTS, BASIS = 4096, 512, 256, 8
PLANES = BASIS + 1
MISH = BASIS
FIRST_PLANE, LAST_PLANE = MISH, BASIS - 1
PAIRS = BASIS // 2
TILES = 4
CHUNK_ROWS = TILES * P
CHUNKS = BATCH // CHUNK_ROWS
COLS = TILES * FEATURES
WORDS = COLS // PACK

ROOT = round(math.sqrt(1.0 / 6.0) * 2**25) / 2**25
MAKE_UP = 1.0 / (6.0 * ROOT * ROOT)

FLOPS = 2 * BATCH * OUTPUTS * PLANES * FEATURES


def tile_net_pa_t_kernel(tc, h1, coef2, sb2, sp2, b2, out):
    nc = tc.nc
    with ExitStack() as stack:
        keep = stack.enter_context(tc.tile_pool(name="keep", bufs=1))
        io = stack.enter_context(tc.tile_pool(name="io", bufs=2))
        work = stack.enter_context(tc.tile_pool(name="work", bufs=2))
        turn_banks = stack.enter_context(tc.psum_pool(name="turn_banks", bufs=2))
        sum_banks = stack.enter_context(tc.psum_pool(name="sum_banks", bufs=1))

        identity = keep.tile([P, P], F32)
        make_identity(nc, identity[:])

        shifts = keep.tile([P, PAIRS + 3], F32)
        for r in range(PAIRS):
            nc.vector.memset(shifts[:, r : r + 1], 1.5 - r)
        nc.vector.memset(shifts[:, PAIRS : PAIRS + 1], -2.0)
        nc.vector.memset(shifts[:, PAIRS + 1 : PAIRS + 2], 1.0)
        minus_two = shifts[:, PAIRS : PAIRS + 1]
        plus_one = shifts[:, PAIRS + 1 : PAIRS + 2]
        nc.vector.memset(shifts[:, PAIRS + 2 : PAIRS + 3], -2.0 * ROOT)
        minus_two_roots = shifts[:, PAIRS + 2 : PAIRS + 3]

        bias = keep.tile([P, OUTPUTS], BF16)
        nc.scalar.dma_start(out=bias[:], in_=b2.partition_broadcast(P))

        w_codes = keep.tile([P, PLANES, OUTPUTS], U32, align_bytes=64)
        w_scales = keep.tile([P, PLANES, OUTPUTS], U8, align_bytes=64)
        with tc.tile_pool(name="wprep", bufs=1) as wprep:
            coef_rows = wprep.tile([P, PACK, OUTPUTS * BASIS], BF16)
            nc.scalar.dma_start(out=coef_rows[:], in_=coef2.rearrange("(p j) o g -> p j (o g)", j=PACK))
            gain_rows = wprep.tile([P, PACK, OUTPUTS], BF16)
            nc.scalar.dma_start(out=gain_rows[:], in_=sp2.rearrange("(p j) o -> p j o", j=PACK))
            base_rows = wprep.tile([P, PACK, OUTPUTS], BF16)
            nc.scalar.dma_start(out=base_rows[:], in_=sb2.rearrange("(p j) o -> p j o", j=PACK))
            w_grouped = wprep.tile([P, PLANES, OUTPUTS, PACK], BF16, align_bytes=64)
            coef_by_plane = coef_rows[:].rearrange("p j (o g) -> p g o j", g=BASIS)
            for g in range(BASIS):
                nc.vector.tensor_tensor(
                    out=w_grouped[:, g],
                    in0=coef_by_plane[:, g],
                    in1=gain_rows[:].rearrange("p j o -> p o j"),
                    op=ALU.mult,
                )
            nc.vector.tensor_copy(out=w_grouped[:, MISH], in_=base_rows[:].rearrange("p j o -> p o j"))
            for plane in range(PLANES):
                nc.vector.quantize_mx(
                    out=w_codes[:, plane, :].bitcast(FP8X4),
                    scales=w_scales[:, plane, :],
                    in_=w_grouped[:, plane].rearrange("p o j -> p (o j)"),
                )

        halves = stack.enter_context(tc.tile_pool(name="halves", bufs=2))
        quant = stack.enter_context(tc.tile_pool(name="quant", bufs=2))
        results = stack.enter_context(tc.tile_pool(name="results", bufs=2))

        def quantise_and_multiply(chunk, plane, values):
            codes, scales, sums = chunk["codes"], chunk["scales"], chunk["sums"]
            nc.vector.quantize_mx(out=codes[:, plane, :].bitcast(FP8X4), scales=scales[:, plane, :], in_=values)
            for t in range(TILES):
                cols = slice(t * P, (t + 1) * P)
                nc.tensor.matmul_mx(
                    out=sums[t][:],
                    lhsT=codes[:, plane, cols].bitcast(FP8X4),
                    lhsT_scale=scales[:, plane, cols],
                    rhs=w_codes[:, plane, :].bitcast(FP8X4),
                    rhs_scale=w_scales[:, plane, :],
                    start=(plane == FIRST_PLANE),
                    stop=(plane == LAST_PLANE),
                )

        def end_at_zero(pair):
            nc.vector.tensor_scalar(
                out=pair["both"][:], in0=pair["both"][:], scalar1=0.0, scalar2=MAKE_UP, op0=ALU.max, op1=ALU.mult
            )

        def take_low(pair):
            nc.vector.tensor_tensor(out=pair["low"][:], in0=pair["both"][:], in1=pair["below"][:], op=ALU.mult)

        def take_high(pair):
            nc.vector.tensor_tensor(out=pair["high"][:], in0=pair["both"][:], in1=pair["low"][:], op=ALU.subtract)

        def finish(pair):
            chunk, r = pair["chunk"], pair["r"]
            quantise_and_multiply(chunk, r, pair["low"][:])
            quantise_and_multiply(chunk, r + PAIRS, pair["high"][:])
            if r == PAIRS - 1:
                result = results.tile([P, TILES, OUTPUTS], F32)
                for t in range(TILES):
                    nc.vector.tensor_tensor(out=result[:, t, :], in0=chunk["sums"][t][:], in1=bias[:], op=ALU.add)
                nc.sync.dma_start(out=out[chunk["rows"], :].rearrange("(p t) o -> p t o", t=TILES), in_=result[:])

        earlier = None
        for c in range(CHUNKS):
            rows = slice(c * CHUNK_ROWS, (c + 1) * CHUNK_ROWS)

            raw = io.tile([P, COLS], BF16)
            nc.sync.dma_start(out=raw[:], in_=h1[rows, :].rearrange("(p t) i -> p (t i)", t=TILES))
            raw_words = raw[:].bitcast(F32).rearrange("p (t w u) -> p t u w", t=TILES, u=2)
            x = io.tile([P, COLS], BF16, align_bytes=64)
            x_words = x[:].bitcast(F32).rearrange("p (h t b u) -> p h t b u", h=2, t=2, u=2)
            for h in range(2):
                turned = turn_banks.tile([P, 2, 2, P], F32)
                for t in range(2):
                    for u in range(2):
                        nc.tensor.transpose(turned[:, t, u, :], raw_words[:, 2 * h + t, u, :], identity[:])
                nc.scalar.copy(out=x_words[:, h], in_=turned[:].rearrange("p t u b -> p t b u"))

            chunk = {
                "rows": rows,
                "codes": quant.tile([P, PLANES, WORDS], U32, align_bytes=64, name="codes"),
                "scales": quant.tile([P, PLANES, WORDS], U8, align_bytes=64, name="scales"),
                "sums": [sum_banks.tile([P, OUTPUTS], F32, name="sum%d" % t) for t in range(TILES)],
            }

            capped = halves.tile([P, COLS], BF16)
            nc.vector.tensor_scalar_min(out=capped[:], in0=x[:], scalar1=20.0)
            soft = work.tile([P, COLS], F32)
            nc.scalar.activation(out=soft[:], in_=capped[:], func=ACT.Exp)
            nc.scalar.activation(out=soft[:], in_=soft[:], func=ACT.Ln, bias=plus_one)
            nc.scalar.activation(out=soft[:], in_=soft[:], func=ACT.Tanh)
            mish = halves.tile([P, COLS], BF16, align_bytes=64)

            for r in range(PAIRS):
                dist = work.tile([P, COLS], F32)
                nc.scalar.activation(out=dist[:], in_=x[:], func=ACT.Abs, scale=1.25, bias=shifts[:, r : r + 1])
                nc.scalar.activation(out=dist[:], in_=dist[:], func=ACT.Abs, bias=minus_two)
                wide = work.tile([P, COLS], F32)
                nc.scalar.activation(out=wide[:], in_=dist[:], func=ACT.Square, scale=ROOT, bias=minus_two_roots)
                narrow = work.tile([P, COLS], F32)
                nc.scalar.activation(
                    out=narrow[:], in_=dist[:], func=ACT.Square, scale=2.0 * ROOT, bias=minus_two_roots
                )
                pair = {
                    "chunk": chunk,
                    "r": r,
                    "both": halves.tile([P, COLS], BF16, name="both"),
                    "below": halves.tile([P, COLS], BF16, name="below"),
                    "low": halves.tile([P, COLS], BF16, align_bytes=64, name="low"),
                    "high": halves.tile([P, COLS], BF16, align_bytes=64, name="high"),
                }
                nc.vector.scalar_tensor_tensor(
                    out=wide[:], in0=dist[:], scalar=-2.0, in1=wide[:], op0=ALU.add, op1=ALU.mult
                )
                if earlier is not None:
                    end_at_zero(earlier)
                nc.vector.scalar_tensor_tensor(
                    out=narrow[:], in0=dist[:], scalar=-1.0, in1=narrow[:], op0=ALU.add, op1=ALU.mult
                )
                if earlier is not None:
                    take_low(earlier)
                nc.vector.tensor_single_scalar(out=pair["below"][:], in_=x[:], scalar=0.8 * r - 1.2, op=ALU.is_lt)
                if earlier is not None:
                    take_high(earlier)
                nc.vector.scalar_tensor_tensor(
                    out=pair["both"][:], in0=narrow[:], scalar=0.0, in1=wide[:], op0=ALU.min, op1=ALU.subtract
                )
                if r == 0:
                    nc.vector.tensor_tensor(out=mish[:], in0=x[:], in1=soft[:], op=ALU.mult)
                if earlier is not None:
                    finish(earlier)
                if r == 0:
                    quantise_and_multiply(chunk, MISH, mish[:])
                earlier = pair

        end_at_zero(earlier)
        take_low(earlier)
        take_high(earlier)
        finish(earlier)
